import numpy as np
import ml_dtypes

BF16 = ml_dtypes.bfloat16


def bf(x):
    return np.asarray(x, np.float32).astype(BF16)


def f32(x):
    return np.asarray(x, np.float32)


def f64(x):
    return np.asarray(x).astype(np.float64)


def striped(idx):
    return np.tile(idx.reshape(-1, 16).T, (8, 1))


C, S, N = 128, 4096, 512


def setup_inputs():
    return {"wt": f32(np.random.standard_normal((C, S))), "s_emb": f32(np.random.standard_normal((C, N))), "a_emb": f32(np.random.standard_normal((C, N))), "rtg": f32(np.random.standard_normal((1, N))), "wr_w": f32(np.random.standard_normal((C, 1))), "wr_b": f32(np.random.standard_normal((C, 1))), "offs": striped(np.random.permutation(np.tile(np.arange(S), 2))[:N])}


def reference(wt, s_emb, a_emb, rtg, wr_w, wr_b, offs):
    idx = offs[:16].T.reshape(-1)
    te = f64(wt)[:, idx]
    re = te + (f64(wr_w) * f64(rtg) + f64(wr_b))
    se = te + f64(s_emb)
    ae = te + f64(a_emb)
    return np.stack((re, se, ae), axis=-1).reshape(C, -1)

@@ -1,0 +1,46 @@
+import concourse.mybir as mybir
+
+C = 128
+S = 4096
+N = 512
+TOKENS = 3
+
+F32 = mybir.dt.float32
+U16 = mybir.dt.uint16
+ADD = mybir.AluOpType.add
+MULT = mybir.AluOpType.mult
+
+
+def tile_decisiontransformer_kernel(tc, wt, s_emb, a_emb, rtg, wr_w, wr_b, offs, out):
+    nc = tc.nc
+    with tc.tile_pool(name="held", bufs=1) as held:
+        offsets = held.tile([C, N // 16], U16, name="offsets")
+        nc.sync.dma_start(offsets[:], offs)
+
+        rtg_rows = held.tile([C, N], F32, name="rtg_rows")
+        nc.scalar.dma_start(rtg_rows[:], rtg.broadcast_to([C, N]))
+        weight = held.tile([C, 1], F32, name="weight")
+        nc.scalar.dma_start(weight[:], wr_w)
+        bias = held.tile([C, 1], F32, name="bias")
+        nc.scalar.dma_start(bias[:], wr_b)
+
+        table = held.tile([C, S], F32, name="table")
+        nc.sync.dma_start(table[:, : S // 2], wt[:, : S // 2])
+        nc.scalar.dma_start(table[:, S // 2 :], wt[:, S // 2 :])
+
+        state = held.tile([C, N], F32, name="state")
+        nc.sync.dma_start(state[:], s_emb)
+        action = held.tile([C, N], F32, name="action")
+        nc.scalar.dma_start(action[:], a_emb)
+
+        ret = held.tile([C, N], F32, name="ret")
+        nc.vector.tensor_scalar(ret[:], rtg_rows[:], weight[:, 0:1], bias[:, 0:1], MULT, ADD)
+
+        sums = held.tile([C, TOKENS, N], F32, name="sums")
+        for k, other in enumerate((ret, state, action)):
+            nc.vector.tensor_tensor(sums[:, k, :], table[:].indirect(offsets[:]), other[:], ADD)
+
+        tokens = held.tile([C, N, TOKENS], F32, name="tokens")
+        nc.scalar.copy(tokens[:], sums[:].rearrange("c k j -> c j k"))
+
+        nc.sync.dma_start(out.rearrange("c (j k) -> c j k", k=TOKENS), tokens[:])

@@ -4,6 +4,8 @@ C = 128
 S = 4096
 N = 512
 TOKENS = 3
+PIECE = 128
+PIECES = N // PIECE
 
 F32 = mybir.dt.float32
 U16 = mybir.dt.uint16
@@ -13,7 +15,10 @@ MULT = mybir.AluOpType.mult
 
 def tile_decisiontransformer_kernel(tc, wt, s_emb, a_emb, rtg, wr_w, wr_b, offs, out):
     nc = tc.nc
-    with tc.tile_pool(name="held", bufs=1) as held:
+    with (
+        tc.tile_pool(name="held", bufs=1) as held,
+        tc.tile_pool(name="ring", bufs=PIECES) as ring,
+    ):
         offsets = held.tile([C, N // 16], U16, name="offsets")
         nc.sync.dma_start(offsets[:], offs)
 
@@ -36,11 +41,18 @@ def tile_decisiontransformer_kernel(tc, wt, s_emb, a_emb, rtg, wr_w, wr_b, offs,
         ret = held.tile([C, N], F32, name="ret")
         nc.vector.tensor_scalar(ret[:], rtg_rows[:], weight[:, 0:1], bias[:, 0:1], MULT, ADD)
 
-        sums = held.tile([C, TOKENS, N], F32, name="sums")
-        for k, other in enumerate((ret, state, action)):
-            nc.vector.tensor_tensor(sums[:, k, :], table[:].indirect(offsets[:]), other[:], ADD)
+        out_steps = out.rearrange("c (j k) -> c j k", k=TOKENS)
+        for p in range(PIECES):
+            steps = slice(p * PIECE, (p + 1) * PIECE)
+            piece_offsets = offsets[:, p * PIECE // 16 : (p + 1) * PIECE // 16]
 
-        tokens = held.tile([C, N, TOKENS], F32, name="tokens")
-        nc.scalar.copy(tokens[:], sums[:].rearrange("c k j -> c j k"))
+            sums = ring.tile([C, TOKENS, PIECE], F32, name="sums")
+            for k, other in enumerate((ret, state, action)):
+                nc.vector.tensor_tensor(
+                    sums[:, k, :], table[:].indirect(piece_offsets), other[:, steps], ADD
+                )
 
-        nc.sync.dma_start(out.rearrange("c (j k) -> c j k", k=TOKENS), tokens[:])
+            tokens = ring.tile([C, PIECE, TOKENS], F32, name="tokens")
+            nc.scalar.copy(tokens[:], sums[:].rearrange("c k j -> c j k"))
+
+            nc.sync.dma_start(out_steps[:, steps, :], tokens[:])

@@ -10,7 +10,6 @@ PIECES = N // PIECE
 F32 = mybir.dt.float32
 U16 = mybir.dt.uint16
 ADD = mybir.AluOpType.add
-MULT = mybir.AluOpType.mult
 
 
 def tile_decisiontransformer_kernel(tc, wt, s_emb, a_emb, rtg, wr_w, wr_b, offs, out):
@@ -18,16 +17,17 @@ def tile_decisiontransformer_kernel(tc, wt, s_emb, a_emb, rtg, wr_w, wr_b, offs,
     with (
         tc.tile_pool(name="held", bufs=1) as held,
         tc.tile_pool(name="ring", bufs=PIECES) as ring,
+        tc.psum_pool(name="psum", bufs=1) as psum,
     ):
         offsets = held.tile([C, N // 16], U16, name="offsets")
         nc.sync.dma_start(offsets[:], offs)
 
-        rtg_rows = held.tile([C, N], F32, name="rtg_rows")
-        nc.scalar.dma_start(rtg_rows[:], rtg.broadcast_to([C, N]))
-        weight = held.tile([C, 1], F32, name="weight")
-        nc.scalar.dma_start(weight[:], wr_w)
-        bias = held.tile([C, 1], F32, name="bias")
-        nc.scalar.dma_start(bias[:], wr_b)
+        projection = held.tile([2, C], F32, name="projection")
+        nc.scalar.dma_start(projection[0:1, :], wr_w.rearrange("c o -> o c"))
+        nc.scalar.dma_start(projection[1:2, :], wr_b.rearrange("c o -> o c"))
+        returns = held.tile([2, N], F32, name="returns")
+        nc.vector.memset(returns[:], 1.0)
+        nc.scalar.dma_start(returns[0:1, :], rtg)
 
         table = held.tile([C, S], F32, name="table")
         nc.sync.dma_start(table[:, : S // 2], wt[:, : S // 2])
@@ -38,8 +38,10 @@ def tile_decisiontransformer_kernel(tc, wt, s_emb, a_emb, rtg, wr_w, wr_b, offs,
         action = held.tile([C, N], F32, name="action")
         nc.scalar.dma_start(action[:], a_emb)
 
+        ret_psum = psum.tile([C, N], F32, name="ret_psum")
+        nc.tensor.matmul(ret_psum[:], projection[:], returns[:], start=True, stop=True)
         ret = held.tile([C, N], F32, name="ret")
-        nc.vector.tensor_scalar(ret[:], rtg_rows[:], weight[:, 0:1], bias[:, 0:1], MULT, ADD)
+        nc.scalar.copy(ret[:], ret_psum[:])
 
         out_steps = out.rearrange("c (j k) -> c j k", k=TOKENS)
         for p in range(PIECES):

@@ -16,18 +16,17 @@ def tile_decisiontransformer_kernel(tc, wt, s_emb, a_emb, rtg, wr_w, wr_b, offs,
     nc = tc.nc
     with (
         tc.tile_pool(name="held", bufs=1) as held,
-        tc.tile_pool(name="ring", bufs=PIECES) as ring,
         tc.psum_pool(name="psum", bufs=1) as psum,
     ):
+        projection = held.tile([2, C], F32, name="projection")
+        nc.scalar.dma_start(projection[0:1, :], wr_b.rearrange("c o -> o c"))
+        nc.scalar.dma_start(projection[1:2, :], wr_w.rearrange("c o -> o c"))
+        returns = held.tile([2, N], F32, name="returns")
+        nc.vector.memset(returns[0:1, :], 1.0)
+        nc.scalar.dma_start(returns[1:2, :], rtg)
+
         offsets = held.tile([C, N // 16], U16, name="offsets")
         nc.sync.dma_start(offsets[:], offs)
-
-        projection = held.tile([2, C], F32, name="projection")
-        nc.scalar.dma_start(projection[0:1, :], wr_w.rearrange("c o -> o c"))
-        nc.scalar.dma_start(projection[1:2, :], wr_b.rearrange("c o -> o c"))
-        returns = held.tile([2, N], F32, name="returns")
-        nc.vector.memset(returns[:], 1.0)
-        nc.scalar.dma_start(returns[0:1, :], rtg)
 
         table = held.tile([C, S], F32, name="table")
         nc.sync.dma_start(table[:, : S // 2], wt[:, : S // 2])
@@ -43,18 +42,19 @@ def tile_decisiontransformer_kernel(tc, wt, s_emb, a_emb, rtg, wr_w, wr_b, offs,
         ret = held.tile([C, N], F32, name="ret")
         nc.scalar.copy(ret[:], ret_psum[:])
 
+        sums = held.tile([C, TOKENS, N], F32, name="sums")
+        tokens = held.tile([C, N, TOKENS], F32, name="tokens")
         out_steps = out.rearrange("c (j k) -> c j k", k=TOKENS)
+
+        nc.vector.tensor_tensor(sums[:, 0, :], table[:].indirect(offsets[:]), ret[:], ADD)
         for p in range(PIECES):
             steps = slice(p * PIECE, (p + 1) * PIECE)
             piece_offsets = offsets[:, p * PIECE // 16 : (p + 1) * PIECE // 16]
-
-            sums = ring.tile([C, TOKENS, PIECE], F32, name="sums")
-            for k, other in enumerate((ret, state, action)):
-                nc.vector.tensor_tensor(
-                    sums[:, k, :], table[:].indirect(piece_offsets), other[:, steps], ADD
-                )
-
-            tokens = ring.tile([C, PIECE, TOKENS], F32, name="tokens")
-            nc.scalar.copy(tokens[:], sums[:].rearrange("c k j -> c j k"))
-
-            nc.sync.dma_start(out_steps[:, steps, :], tokens[:])
+            nc.vector.tensor_tensor(
+                sums[:, 1, steps], table[:].indirect(piece_offsets), state[:, steps], ADD
+            )
+            nc.vector.tensor_tensor(
+                sums[:, 2, steps], table[:].indirect(piece_offsets), action[:, steps], ADD
+            )
+            nc.scalar.copy(tokens[:, steps, :], sums[:, :, steps].rearrange("c k j -> c j k"))
+            nc.sync.dma_start(out_steps[:, steps, :], tokens[:, steps, :])

@@ -23,7 +23,7 @@ def tile_decisiontransformer_kernel(tc, wt, s_emb, a_emb, rtg, wr_w, wr_b, offs,
         nc.scalar.dma_start(projection[1:2, :], wr_w.rearrange("c o -> o c"))
         returns = held.tile([2, N], F32, name="returns")
         nc.vector.memset(returns[0:1, :], 1.0)
-        nc.scalar.dma_start(returns[1:2, :], rtg)
+        nc.sync.dma_start(returns[1:2, :], rtg)
 
         offsets = held.tile([C, N // 16], U16, name="offsets")
         nc.sync.dma_start(offsets[:], offs)

@@ -16,7 +16,8 @@ def tile_decisiontransformer_kernel(tc, wt, s_emb, a_emb, rtg, wr_w, wr_b, offs,
     nc = tc.nc
     with (
         tc.tile_pool(name="held", bufs=1) as held,
-        tc.psum_pool(name="psum", bufs=1) as psum,
+        tc.tile_pool(name="ring", bufs=PIECES) as ring,
+        tc.psum_pool(name="psum", bufs=PIECES) as psum,
     ):
         projection = held.tile([2, C], F32, name="projection")
         nc.scalar.dma_start(projection[0:1, :], wr_b.rearrange("c o -> o c"))
@@ -37,24 +38,30 @@ def tile_decisiontransformer_kernel(tc, wt, s_emb, a_emb, rtg, wr_w, wr_b, offs,
         action = held.tile([C, N], F32, name="action")
         nc.scalar.dma_start(action[:], a_emb)
 
-        ret_psum = psum.tile([C, N], F32, name="ret_psum")
-        nc.tensor.matmul(ret_psum[:], projection[:], returns[:], start=True, stop=True)
-        ret = held.tile([C, N], F32, name="ret")
-        nc.scalar.copy(ret[:], ret_psum[:])
+        def looked_up(p):
+            return table[:].indirect(offsets[:, p * PIECE // 16 : (p + 1) * PIECE // 16])
 
-        sums = held.tile([C, TOKENS, N], F32, name="sums")
-        tokens = held.tile([C, N, TOKENS], F32, name="tokens")
-        out_steps = out.rearrange("c (j k) -> c j k", k=TOKENS)
-
-        nc.vector.tensor_tensor(sums[:, 0, :], table[:].indirect(offsets[:]), ret[:], ADD)
+        sums_of = []
         for p in range(PIECES):
             steps = slice(p * PIECE, (p + 1) * PIECE)
-            piece_offsets = offsets[:, p * PIECE // 16 : (p + 1) * PIECE // 16]
-            nc.vector.tensor_tensor(
-                sums[:, 1, steps], table[:].indirect(piece_offsets), state[:, steps], ADD
-            )
-            nc.vector.tensor_tensor(
-                sums[:, 2, steps], table[:].indirect(piece_offsets), action[:, steps], ADD
-            )
-            nc.scalar.copy(tokens[:, steps, :], sums[:, :, steps].rearrange("c k j -> c j k"))
-            nc.sync.dma_start(out_steps[:, steps, :], tokens[:, steps, :])
+
+            ret_psum = psum.tile([C, PIECE], F32, name="ret_psum")
+            nc.tensor.matmul(ret_psum[:], projection[:], returns[:, steps], start=True, stop=True)
+            ret = ring.tile([C, PIECE], F32, name="ret")
+            nc.scalar.copy(ret[:], ret_psum[:])
+
+            sums = ring.tile([C, TOKENS, PIECE], F32, name="sums")
+            nc.vector.tensor_tensor(sums[:, 0, :], looked_up(p), ret[:], ADD)
+            sums_of.append(sums)
+
+        out_steps = out.rearrange("c (j k) -> c j k", k=TOKENS)
+        for p in range(PIECES):
+            steps = slice(p * PIECE, (p + 1) * PIECE)
+            sums = sums_of[p]
+            nc.vector.tensor_tensor(sums[:, 1, :], looked_up(p), state[:, steps], ADD)
+            nc.vector.tensor_tensor(sums[:, 2, :], looked_up(p), action[:, steps], ADD)
+
+            tokens = ring.tile([C, PIECE, TOKENS], F32, name="tokens")
+            nc.scalar.copy(tokens[:], sums[:].rearrange("c k j -> c j k"))
+
+            nc.sync.dma_start(out_steps[:, steps, :], tokens[:])

@@ -62,6 +62,7 @@ def tile_decisiontransformer_kernel(tc, wt, s_emb, a_emb, rtg, wr_w, wr_b, offs,
             nc.vector.tensor_tensor(sums[:, 2, :], looked_up(p), action[:, steps], ADD)
 
             tokens = ring.tile([C, PIECE, TOKENS], F32, name="tokens")
-            nc.scalar.copy(tokens[:], sums[:].rearrange("c k j -> c j k"))
+            interleave = nc.scalar.copy if p < PIECES - 1 else nc.vector.tensor_copy
+            interleave(tokens[:], sums[:].rearrange("c k j -> c j k"))
 
             nc.sync.dma_start(out_steps[:, steps, :], tokens[:])

@@ -48,7 +48,7 @@ def tile_decisiontransformer_kernel(tc, wt, s_emb, a_emb, rtg, wr_w, wr_b, offs,
             ret_psum = psum.tile([C, PIECE], F32, name="ret_psum")
             nc.tensor.matmul(ret_psum[:], projection[:], returns[:, steps], start=True, stop=True)
             ret = ring.tile([C, PIECE], F32, name="ret")
-            nc.scalar.copy(ret[:], ret_psum[:])
+            nc.vector.tensor_copy(ret[:], ret_psum[:])
 
             sums = ring.tile([C, TOKENS, PIECE], F32, name="sums")
             nc.vector.tensor_tensor(sums[:, 0, :], looked_up(p), ret[:], ADD)

@@ -41,28 +41,24 @@ def tile_decisiontransformer_kernel(tc, wt, s_emb, a_emb, rtg, wr_w, wr_b, offs,
         def looked_up(p):
             return table[:].indirect(offsets[:, p * PIECE // 16 : (p + 1) * PIECE // 16])
 
-        sums_of = []
+        ret = held.tile([C, N], F32, name="ret")
         for p in range(PIECES):
             steps = slice(p * PIECE, (p + 1) * PIECE)
-
             ret_psum = psum.tile([C, PIECE], F32, name="ret_psum")
             nc.tensor.matmul(ret_psum[:], projection[:], returns[:, steps], start=True, stop=True)
-            ret = ring.tile([C, PIECE], F32, name="ret")
-            nc.vector.tensor_copy(ret[:], ret_psum[:])
+            nc.vector.tensor_copy(ret[:, steps], ret_psum[:])
 
-            sums = ring.tile([C, TOKENS, PIECE], F32, name="sums")
-            nc.vector.tensor_tensor(sums[:, 0, :], looked_up(p), ret[:], ADD)
-            sums_of.append(sums)
+        sums = held.tile([C, TOKENS, N], F32, name="sums")
+        nc.vector.tensor_tensor(sums[:, 0, :], table[:].indirect(offsets[:]), ret[:], ADD)
 
         out_steps = out.rearrange("c (j k) -> c j k", k=TOKENS)
         for p in range(PIECES):
             steps = slice(p * PIECE, (p + 1) * PIECE)
-            sums = sums_of[p]
-            nc.vector.tensor_tensor(sums[:, 1, :], looked_up(p), state[:, steps], ADD)
-            nc.vector.tensor_tensor(sums[:, 2, :], looked_up(p), action[:, steps], ADD)
+            nc.vector.tensor_tensor(sums[:, 1, steps], looked_up(p), state[:, steps], ADD)
+            nc.vector.tensor_tensor(sums[:, 2, steps], looked_up(p), action[:, steps], ADD)
 
             tokens = ring.tile([C, PIECE, TOKENS], F32, name="tokens")
             interleave = nc.scalar.copy if p < PIECES - 1 else nc.vector.tensor_copy
-            interleave(tokens[:], sums[:].rearrange("c k j -> c j k"))
+            interleave(tokens[:], sums[:, :, steps].rearrange("c k j -> c j k"))
 
             nc.sync.dma_start(out_steps[:, steps, :], tokens[:])

@@ -58,7 +58,12 @@ def tile_decisiontransformer_kernel(tc, wt, s_emb, a_emb, rtg, wr_w, wr_b, offs,
             nc.vector.tensor_tensor(sums[:, 2, steps], looked_up(p), action[:, steps], ADD)
 
             tokens = ring.tile([C, PIECE, TOKENS], F32, name="tokens")
-            interleave = nc.scalar.copy if p < PIECES - 1 else nc.vector.tensor_copy
-            interleave(tokens[:], sums[:, :, steps].rearrange("c k j -> c j k"))
-
-            nc.sync.dma_start(out_steps[:, steps, :], tokens[:])
+            if p < PIECES - 1:
+                nc.scalar.copy(tokens[:], sums[:, :, steps].rearrange("c k j -> c j k"))
+                nc.sync.dma_start(out_steps[:, steps, :], tokens[:])
+            else:
+                for h in range(2):
+                    local = slice(h * PIECE // 2, (h + 1) * PIECE // 2)
+                    half = slice(steps.start + local.start, steps.start + local.stop)
+                    nc.vector.tensor_copy(tokens[:, local, :], sums[:, :, half].rearrange("c k j -> c j k"))
+                    nc.sync.dma_start(out_steps[:, half, :], tokens[:, local, :])

@@ -58,12 +58,10 @@ def tile_decisiontransformer_kernel(tc, wt, s_emb, a_emb, rtg, wr_w, wr_b, offs,
             nc.vector.tensor_tensor(sums[:, 2, steps], looked_up(p), action[:, steps], ADD)
 
             tokens = ring.tile([C, PIECE, TOKENS], F32, name="tokens")
-            if p < PIECES - 1:
-                nc.scalar.copy(tokens[:], sums[:, :, steps].rearrange("c k j -> c j k"))
-                nc.sync.dma_start(out_steps[:, steps, :], tokens[:])
-            else:
-                for h in range(2):
-                    local = slice(h * PIECE // 2, (h + 1) * PIECE // 2)
-                    half = slice(steps.start + local.start, steps.start + local.stop)
-                    nc.vector.tensor_copy(tokens[:, local, :], sums[:, :, half].rearrange("c k j -> c j k"))
-                    nc.sync.dma_start(out_steps[:, half, :], tokens[:, local, :])
+            interleave = nc.scalar.copy if p < PIECES - 1 else nc.vector.tensor_copy
+            parts = 1 if p < PIECES - 2 else 2
+            for h in range(parts):
+                local = slice(h * PIECE // parts, (h + 1) * PIECE // parts)
+                part = slice(steps.start + local.start, steps.start + local.stop)
+                interleave(tokens[:, local, :], sums[:, :, part].rearrange("c k j -> c j k"))
+                nc.sync.dma_start(out_steps[:, part, :], tokens[:, local, :])

@@ -17,7 +17,7 @@ def tile_decisiontransformer_kernel(tc, wt, s_emb, a_emb, rtg, wr_w, wr_b, offs,
     with (
         tc.tile_pool(name="held", bufs=1) as held,
         tc.tile_pool(name="ring", bufs=PIECES) as ring,
-        tc.psum_pool(name="psum", bufs=PIECES) as psum,
+        tc.psum_pool(name="psum", bufs=1) as psum,
     ):
         projection = held.tile([2, C], F32, name="projection")
         nc.scalar.dma_start(projection[0:1, :], wr_b.rearrange("c o -> o c"))
@@ -41,12 +41,10 @@ def tile_decisiontransformer_kernel(tc, wt, s_emb, a_emb, rtg, wr_w, wr_b, offs,
         def looked_up(p):
             return table[:].indirect(offsets[:, p * PIECE // 16 : (p + 1) * PIECE // 16])
 
+        ret_psum = psum.tile([C, N], F32, name="ret_psum")
+        nc.tensor.matmul(ret_psum[:], projection[:], returns[:], start=True, stop=True)
         ret = held.tile([C, N], F32, name="ret")
-        for p in range(PIECES):
-            steps = slice(p * PIECE, (p + 1) * PIECE)
-            ret_psum = psum.tile([C, PIECE], F32, name="ret_psum")
-            nc.tensor.matmul(ret_psum[:], projection[:], returns[:, steps], start=True, stop=True)
-            nc.vector.tensor_copy(ret[:, steps], ret_psum[:])
+        nc.vector.tensor_copy(ret[:], ret_psum[:])
 
         sums = held.tile([C, TOKENS, N], F32, name="sums")
         nc.vector.tensor_tensor(sums[:, 0, :], table[:].indirect(offsets[:]), ret[:], ADD)

@@ -57,7 +57,7 @@ def tile_decisiontransformer_kernel(tc, wt, s_emb, a_emb, rtg, wr_w, wr_b, offs,
 
             tokens = ring.tile([C, PIECE, TOKENS], F32, name="tokens")
             interleave = nc.scalar.copy if p < PIECES - 1 else nc.vector.tensor_copy
-            parts = 1 if p < PIECES - 2 else 2
+            parts = 2
             for h in range(parts):
                 local = slice(h * PIECE // parts, (h + 1) * PIECE // parts)
                 part = slice(steps.start + local.start, steps.start + local.stop)

@@ -6,6 +6,7 @@ N = 512
 TOKENS = 3
 PIECE = 128
 PIECES = N // PIECE
+HALF = PIECE // 2
 
 F32 = mybir.dt.float32
 U16 = mybir.dt.uint16
@@ -19,12 +20,13 @@ def tile_decisiontransformer_kernel(tc, wt, s_emb, a_emb, rtg, wr_w, wr_b, offs,
         tc.tile_pool(name="ring", bufs=PIECES) as ring,
         tc.psum_pool(name="psum", bufs=1) as psum,
     ):
-        projection = held.tile([2, C], F32, name="projection")
-        nc.scalar.dma_start(projection[0:1, :], wr_b.rearrange("c o -> o c"))
-        nc.scalar.dma_start(projection[1:2, :], wr_w.rearrange("c o -> o c"))
-        returns = held.tile([2, N], F32, name="returns")
-        nc.vector.memset(returns[0:1, :], 1.0)
-        nc.sync.dma_start(returns[1:2, :], rtg)
+
+        bias_and_weight = held.tile([2, C], F32, name="bias_and_weight")
+        nc.scalar.dma_start(bias_and_weight[0:1, :], wr_b.rearrange("c o -> o c"))
+        nc.scalar.dma_start(bias_and_weight[1:2, :], wr_w.rearrange("c o -> o c"))
+        ones_and_rtg = held.tile([2, N], F32, name="ones_and_rtg")
+        nc.vector.memset(ones_and_rtg[0:1, :], 1.0)
+        nc.sync.dma_start(ones_and_rtg[1:2, :], rtg)
 
         offsets = held.tile([C, N // 16], U16, name="offsets")
         nc.sync.dma_start(offsets[:], offs)
@@ -38,28 +40,24 @@ def tile_decisiontransformer_kernel(tc, wt, s_emb, a_emb, rtg, wr_w, wr_b, offs,
         action = held.tile([C, N], F32, name="action")
         nc.scalar.dma_start(action[:], a_emb)
 
-        def looked_up(p):
-            return table[:].indirect(offsets[:, p * PIECE // 16 : (p + 1) * PIECE // 16])
-
-        ret_psum = psum.tile([C, N], F32, name="ret_psum")
-        nc.tensor.matmul(ret_psum[:], projection[:], returns[:], start=True, stop=True)
-        ret = held.tile([C, N], F32, name="ret")
-        nc.vector.tensor_copy(ret[:], ret_psum[:])
+        projected_psum = psum.tile([C, N], F32, name="projected_psum")
+        nc.tensor.matmul(projected_psum[:], bias_and_weight[:], ones_and_rtg[:], start=True, stop=True)
+        projected = held.tile([C, N], F32, name="projected")
+        nc.vector.tensor_copy(projected[:], projected_psum[:])
 
         sums = held.tile([C, TOKENS, N], F32, name="sums")
-        nc.vector.tensor_tensor(sums[:, 0, :], table[:].indirect(offsets[:]), ret[:], ADD)
+        nc.vector.tensor_tensor(sums[:, 0, :], table[:].indirect(offsets[:]), projected[:], ADD)
 
         out_steps = out.rearrange("c (j k) -> c j k", k=TOKENS)
         for p in range(PIECES):
             steps = slice(p * PIECE, (p + 1) * PIECE)
-            nc.vector.tensor_tensor(sums[:, 1, steps], looked_up(p), state[:, steps], ADD)
-            nc.vector.tensor_tensor(sums[:, 2, steps], looked_up(p), action[:, steps], ADD)
+            looked_up = table[:].indirect(offsets[:, steps.start // 16 : steps.stop // 16])
+            nc.vector.tensor_tensor(sums[:, 1, steps], looked_up, state[:, steps], ADD)
+            nc.vector.tensor_tensor(sums[:, 2, steps], looked_up, action[:, steps], ADD)
 
-            tokens = ring.tile([C, PIECE, TOKENS], F32, name="tokens")
             interleave = nc.scalar.copy if p < PIECES - 1 else nc.vector.tensor_copy
-            parts = 2
-            for h in range(parts):
-                local = slice(h * PIECE // parts, (h + 1) * PIECE // parts)
-                part = slice(steps.start + local.start, steps.start + local.stop)
-                interleave(tokens[:, local, :], sums[:, :, part].rearrange("c k j -> c j k"))
-                nc.sync.dma_start(out_steps[:, part, :], tokens[:, local, :])
+            tokens = ring.tile([C, PIECE, TOKENS], F32, name="tokens")
+            for in_piece in (slice(0, HALF), slice(HALF, PIECE)):
+                in_list = slice(steps.start + in_piece.start, steps.start + in_piece.stop)
+                interleave(tokens[:, in_piece, :], sums[:, :, in_list].rearrange("c k j -> c j k"))
+                nc.sync.dma_start(out_steps[:, in_list, :], tokens[:, in_piece, :])

@@ -20,19 +20,19 @@ def tile_decisiontransformer_kernel(tc, wt, s_emb, a_emb, rtg, wr_w, wr_b, offs,
         tc.tile_pool(name="ring", bufs=PIECES) as ring,
         tc.psum_pool(name="psum", bufs=1) as psum,
     ):
-
-        bias_and_weight = held.tile([2, C], F32, name="bias_and_weight")
-        nc.scalar.dma_start(bias_and_weight[0:1, :], wr_b.rearrange("c o -> o c"))
-        nc.scalar.dma_start(bias_and_weight[1:2, :], wr_w.rearrange("c o -> o c"))
-        ones_and_rtg = held.tile([2, N], F32, name="ones_and_rtg")
-        nc.vector.memset(ones_and_rtg[0:1, :], 1.0)
-        nc.sync.dma_start(ones_and_rtg[1:2, :], rtg)
-
-        offsets = held.tile([C, N // 16], U16, name="offsets")
-        nc.sync.dma_start(offsets[:], offs)
+        rtg_row = held.tile([1, N], F32, name="rtg_row")
+        nc.sync.dma_start(rtg_row[:], rtg)
+        weight_row = held.tile([1, C], F32, name="weight_row")
+        nc.scalar.dma_start(weight_row[:], wr_w.rearrange("c o -> o c"))
 
         table = held.tile([C, S], F32, name="table")
         nc.sync.dma_start(table[:, : S // 2], wt[:, : S // 2])
+
+        bias = held.tile([C, 1], F32, name="bias")
+        nc.scalar.dma_start(bias[:], wr_b)
+        offsets = held.tile([C, N // 16], U16, name="offsets")
+        nc.sync.dma_start(offsets[:], offs)
+
         nc.scalar.dma_start(table[:, S // 2 :], wt[:, S // 2 :])
 
         state = held.tile([C, N], F32, name="state")
@@ -40,10 +40,10 @@ def tile_decisiontransformer_kernel(tc, wt, s_emb, a_emb, rtg, wr_w, wr_b, offs,
         action = held.tile([C, N], F32, name="action")
         nc.scalar.dma_start(action[:], a_emb)
 
-        projected_psum = psum.tile([C, N], F32, name="projected_psum")
-        nc.tensor.matmul(projected_psum[:], bias_and_weight[:], ones_and_rtg[:], start=True, stop=True)
+        product = psum.tile([C, N], F32, name="product")
+        nc.tensor.matmul(product[:], weight_row[:], rtg_row[:], start=True, stop=True)
         projected = held.tile([C, N], F32, name="projected")
-        nc.vector.tensor_copy(projected[:], projected_psum[:])
+        nc.vector.tensor_scalar(projected[:], product[:], bias[:], None, op0=ADD)
 
         sums = held.tile([C, TOKENS, N], F32, name="sums")
         nc.vector.tensor_tensor(sums[:, 0, :], table[:].indirect(offsets[:]), projected[:], ADD)

@@ -28,8 +28,8 @@ def tile_decisiontransformer_kernel(tc, wt, s_emb, a_emb, rtg, wr_w, wr_b, offs,
         table = held.tile([C, S], F32, name="table")
         nc.sync.dma_start(table[:, : S // 2], wt[:, : S // 2])
 
-        bias = held.tile([C, 1], F32, name="bias")
-        nc.scalar.dma_start(bias[:], wr_b)
+        bias_row = held.tile([1, C], F32, name="bias_row")
+        nc.scalar.dma_start(bias_row[:], wr_b.rearrange("c o -> o c"))
         offsets = held.tile([C, N // 16], U16, name="offsets")
         nc.sync.dma_start(offsets[:], offs)
 
@@ -42,6 +42,10 @@ def tile_decisiontransformer_kernel(tc, wt, s_emb, a_emb, rtg, wr_w, wr_b, offs,
 
         product = psum.tile([C, N], F32, name="product")
         nc.tensor.matmul(product[:], weight_row[:], rtg_row[:], start=True, stop=True)
+        one = held.tile([1, 1], F32, name="one")
+        nc.vector.memset(one[:], 1.0)
+        bias = psum.tile([C, 1], F32, name="bias")
+        nc.tensor.matmul(bias[:], bias_row[:], one[:], start=True, stop=True)
         projected = held.tile([C, N], F32, name="projected")
         nc.vector.tensor_scalar(projected[:], product[:], bias[:], None, op0=ADD)
 

@@ -20,9 +20,9 @@ def tile_decisiontransformer_kernel(tc, wt, s_emb, a_emb, rtg, wr_w, wr_b, offs,
         tc.tile_pool(name="ring", bufs=PIECES) as ring,
         tc.psum_pool(name="psum", bufs=1) as psum,
     ):
-        rtg_row = held.tile([1, N], F32, name="rtg_row")
+        rtg_row = held.tile([1, N], F32, name="rtg_row", tag="rtg_then_state")
         nc.sync.dma_start(rtg_row[:], rtg)
-        weight_row = held.tile([1, C], F32, name="weight_row")
+        weight_row = held.tile([1, C], F32, name="weight_row", tag="weight_then_action")
         nc.scalar.dma_start(weight_row[:], wr_w.rearrange("c o -> o c"))
 
         table = held.tile([C, S], F32, name="table")
@@ -35,13 +35,14 @@ def tile_decisiontransformer_kernel(tc, wt, s_emb, a_emb, rtg, wr_w, wr_b, offs,
 
         nc.scalar.dma_start(table[:, S // 2 :], wt[:, S // 2 :])
 
-        state = held.tile([C, N], F32, name="state")
-        nc.sync.dma_start(state[:], s_emb)
-        action = held.tile([C, N], F32, name="action")
-        nc.scalar.dma_start(action[:], a_emb)
-
         product = psum.tile([C, N], F32, name="product")
         nc.tensor.matmul(product[:], weight_row[:], rtg_row[:], start=True, stop=True)
+
+        state = held.tile([C, N], F32, name="state", tag="rtg_then_state")
+        nc.sync.dma_start(state[:], s_emb)
+        action = held.tile([C, N], F32, name="action", tag="weight_then_action")
+        nc.scalar.dma_start(action[:], a_emb)
+
         one = held.tile([1, 1], F32, name="one")
         nc.vector.memset(one[:], 1.0)
         bias = psum.tile([C, 1], F32, name="bias")

@@ -22,31 +22,32 @@ def tile_decisiontransformer_kernel(tc, wt, s_emb, a_emb, rtg, wr_w, wr_b, offs,
     ):
         rtg_row = held.tile([1, N], F32, name="rtg_row", tag="rtg_then_state")
         nc.sync.dma_start(rtg_row[:], rtg)
-        weight_row = held.tile([1, C], F32, name="weight_row", tag="weight_then_action")
+        weight_row = held.tile([1, C], F32, name="weight_row")
         nc.scalar.dma_start(weight_row[:], wr_w.rearrange("c o -> o c"))
 
         table = held.tile([C, S], F32, name="table")
         nc.sync.dma_start(table[:, : S // 2], wt[:, : S // 2])
 
-        bias_row = held.tile([1, C], F32, name="bias_row")
+        bias_row = held.tile([1, C], F32, name="bias_row", tag="bias_then_action")
         nc.scalar.dma_start(bias_row[:], wr_b.rearrange("c o -> o c"))
         offsets = held.tile([C, N // 16], U16, name="offsets")
         nc.sync.dma_start(offsets[:], offs)
 
-        nc.scalar.dma_start(table[:, S // 2 :], wt[:, S // 2 :])
+        nc.sync.dma_start(table[:, S // 2 :], wt[:, S // 2 :])
 
         product = psum.tile([C, N], F32, name="product")
         nc.tensor.matmul(product[:], weight_row[:], rtg_row[:], start=True, stop=True)
-
-        state = held.tile([C, N], F32, name="state", tag="rtg_then_state")
-        nc.sync.dma_start(state[:], s_emb)
-        action = held.tile([C, N], F32, name="action", tag="weight_then_action")
-        nc.scalar.dma_start(action[:], a_emb)
 
         one = held.tile([1, 1], F32, name="one")
         nc.vector.memset(one[:], 1.0)
         bias = psum.tile([C, 1], F32, name="bias")
         nc.tensor.matmul(bias[:], bias_row[:], one[:], start=True, stop=True)
+
+        state = held.tile([C, N], F32, name="state", tag="rtg_then_state")
+        nc.sync.dma_start(state[:], s_emb)
+        action = held.tile([C, N], F32, name="action", tag="bias_then_action")
+        nc.scalar.dma_start(action[:], a_emb)
+
         projected = held.tile([C, N], F32, name="projected")
         nc.vector.tensor_scalar(projected[:], product[:], bias[:], None, op0=ADD)
 

@@ -26,14 +26,12 @@ def tile_decisiontransformer_kernel(tc, wt, s_emb, a_emb, rtg, wr_w, wr_b, offs,
         nc.scalar.dma_start(weight_row[:], wr_w.rearrange("c o -> o c"))
 
         table = held.tile([C, S], F32, name="table")
-        nc.sync.dma_start(table[:, : S // 2], wt[:, : S // 2])
+        nc.sync.dma_start(table[:], wt)
 
         bias_row = held.tile([1, C], F32, name="bias_row", tag="bias_then_action")
         nc.scalar.dma_start(bias_row[:], wr_b.rearrange("c o -> o c"))
         offsets = held.tile([C, N // 16], U16, name="offsets")
         nc.sync.dma_start(offsets[:], offs)
-
-        nc.sync.dma_start(table[:, S // 2 :], wt[:, S // 2 :])
 
         product = psum.tile([C, N], F32, name="product")
         nc.tensor.matmul(product[:], weight_row[:], rtg_row[:], start=True, stop=True)

@@ -20,7 +20,7 @@ def tile_decisiontransformer_kernel(tc, wt, s_emb, a_emb, rtg, wr_w, wr_b, offs,
         tc.tile_pool(name="ring", bufs=PIECES) as ring,
         tc.psum_pool(name="psum", bufs=1) as psum,
     ):
-        rtg_row = held.tile([1, N], F32, name="rtg_row", tag="rtg_then_state")
+        rtg_row = held.tile([1, N], F32, name="rtg_row")
         nc.sync.dma_start(rtg_row[:], rtg)
         weight_row = held.tile([1, C], F32, name="weight_row")
         nc.scalar.dma_start(weight_row[:], wr_w.rearrange("c o -> o c"))
@@ -28,26 +28,28 @@ def tile_decisiontransformer_kernel(tc, wt, s_emb, a_emb, rtg, wr_w, wr_b, offs,
         table = held.tile([C, S], F32, name="table")
         nc.sync.dma_start(table[:], wt)
 
-        bias_row = held.tile([1, C], F32, name="bias_row", tag="bias_then_action")
+        bias_row = held.tile([1, C], F32, name="bias_row")
         nc.scalar.dma_start(bias_row[:], wr_b.rearrange("c o -> o c"))
         offsets = held.tile([C, N // 16], U16, name="offsets")
         nc.sync.dma_start(offsets[:], offs)
+        state = held.tile([C, N], F32, name="state")
+        nc.sync.dma_start(state[:], s_emb)
 
         product = psum.tile([C, N], F32, name="product")
         nc.tensor.matmul(product[:], weight_row[:], rtg_row[:], start=True, stop=True)
 
         one = held.tile([1, 1], F32, name="one")
         nc.vector.memset(one[:], 1.0)
-        bias = psum.tile([C, 1], F32, name="bias")
-        nc.tensor.matmul(bias[:], bias_row[:], one[:], start=True, stop=True)
-
-        state = held.tile([C, N], F32, name="state", tag="rtg_then_state")
-        nc.sync.dma_start(state[:], s_emb)
-        action = held.tile([C, N], F32, name="action", tag="bias_then_action")
-        nc.scalar.dma_start(action[:], a_emb)
+        bias_psum = psum.tile([C, 1], F32, name="bias_psum")
+        nc.tensor.matmul(bias_psum[:], bias_row[:], one[:], start=True, stop=True)
+        bias = held.tile([C, 1], F32, name="bias", tag="bias_then_action")
+        nc.vector.tensor_copy(bias[:], bias_psum[:])
 
         projected = held.tile([C, N], F32, name="projected")
         nc.vector.tensor_scalar(projected[:], product[:], bias[:], None, op0=ADD)
+
+        action = held.tile([C, N], F32, name="action", tag="bias_then_action")
+        nc.scalar.dma_start(action[:], a_emb)
 
         sums = held.tile([C, TOKENS, N], F32, name="sums")
         nc.vector.tensor_tensor(sums[:, 0, :], table[:].indirect(offsets[:]), projected[:], ADD)

import concourse.mybir as mybir

C = 128
S = 4096
N = 512
TOKENS = 3
PIECE = 128
PIECES = N // PIECE
HALF = PIECE // 2

F32 = mybir.dt.float32
U16 = mybir.dt.uint16
ADD = mybir.AluOpType.add


def tile_decisiontransformer_kernel(tc, wt, s_emb, a_emb, rtg, wr_w, wr_b, offs, out):
    nc = tc.nc
    with (
        tc.tile_pool(name="held", bufs=1) as held,
        tc.tile_pool(name="ring", bufs=PIECES) as ring,
        tc.psum_pool(name="psum", bufs=1) as psum,
    ):
        rtg_row = held.tile([1, N], F32, name="rtg_row")
        nc.sync.dma_start(rtg_row[:], rtg)
        weight_row = held.tile([1, C], F32, name="weight_row")
        nc.scalar.dma_start(weight_row[:], wr_w.rearrange("c o -> o c"))

        table = held.tile([C, S], F32, name="table")
        nc.sync.dma_start(table[:], wt)

        bias_row = held.tile([1, C], F32, name="bias_row")
        nc.scalar.dma_start(bias_row[:], wr_b.rearrange("c o -> o c"))
        offsets = held.tile([C, N // 16], U16, name="offsets")
        nc.sync.dma_start(offsets[:], offs)
        state = held.tile([C, N], F32, name="state")
        nc.sync.dma_start(state[:], s_emb)

        product = psum.tile([C, N], F32, name="product")
        nc.tensor.matmul(product[:], weight_row[:], rtg_row[:], start=True, stop=True)

        one = held.tile([1, 1], F32, name="one")
        nc.vector.memset(one[:], 1.0)
        bias_psum = psum.tile([C, 1], F32, name="bias_psum")
        nc.tensor.matmul(bias_psum[:], bias_row[:], one[:], start=True, stop=True)
        bias = held.tile([C, 1], F32, name="bias", tag="bias_then_action")
        nc.vector.tensor_copy(bias[:], bias_psum[:])

        projected = held.tile([C, N], F32, name="projected")
        nc.vector.tensor_scalar(projected[:], product[:], bias[:], None, op0=ADD)

        action = held.tile([C, N], F32, name="action", tag="bias_then_action")
        nc.scalar.dma_start(action[:], a_emb)

        sums = held.tile([C, TOKENS, N], F32, name="sums")
        nc.vector.tensor_tensor(sums[:, 0, :], table[:].indirect(offsets[:]), projected[:], ADD)

        out_steps = out.rearrange("c (j k) -> c j k", k=TOKENS)
        for p in range(PIECES):
            steps = slice(p * PIECE, (p + 1) * PIECE)
            looked_up = table[:].indirect(offsets[:, steps.start // 16 : steps.stop // 16])
            nc.vector.tensor_tensor(sums[:, 1, steps], looked_up, state[:, steps], ADD)
            nc.vector.tensor_tensor(sums[:, 2, steps], looked_up, action[:, steps], ADD)

            interleave = nc.scalar.copy if p < PIECES - 1 else nc.vector.tensor_copy
            tokens = ring.tile([C, PIECE, TOKENS], F32, name="tokens")
            for in_piece in (slice(0, HALF), slice(HALF, PIECE)):
                in_list = slice(steps.start + in_piece.start, steps.start + in_piece.stop)
                interleave(tokens[:, in_piece, :], sums[:, :, in_list].rearrange("c k j -> c j k"))
                nc.sync.dma_start(out_steps[:, in_list, :], tokens[:, in_piece, :])
